import numpy as np
import ml_dtypes


def mxq(x, axis, fmt="e4m3"):
    dtype, down = {"e4m3": (ml_dtypes.float8_e4m3fn, 7), "e5m2": (ml_dtypes.float8_e5m2, 14)}[fmt]
    v = np.moveaxis(np.asarray(x, np.float32).astype(ml_dtypes.bfloat16).astype(np.float64), axis, -1)
    blocks = v.reshape(v.shape[:-1] + (-1, 32))
    amax = np.abs(blocks).max(-1, keepdims=True)
    byte = np.maximum(np.where(amax > 0, np.frexp(amax)[1] - 1 + 127, 0) - down, 1)
    scale = np.exp2(byte - 127.0)
    codes = (blocks / scale).astype(np.float32).astype(dtype).astype(np.float64)
    return np.moveaxis((codes * scale).reshape(v.shape), -1, axis)


WIDE = False


def mx_kscale(k):
    if not WIDE:
        return np.ones(k)
    levels = np.array([10, -10, 5, -5, 0])
    if k % 512:
        return np.exp2(np.random.permutation(np.resize(levels, k // 32))).repeat(32)
    a = np.empty((k // 512, 16))
    for p in range(k // 512):
        a[p, :8] = np.random.permutation(np.resize(levels, 8))
        for g in range(8):
            far = levels[np.abs(levels - a[p, g]) >= 10]
            a[p, g + 8] = far[np.random.randint(len(far))]
    return np.exp2(a.ravel()).repeat(32)


BF16 = ml_dtypes.bfloat16


def bf(x):
    return np.asarray(x, np.float32).astype(BF16)


def f64(x):
    return np.asarray(x).astype(np.float64)


E2M1 = np.array([0.0, 0.5, 1.0, 1.5, 2.0, 3.0, 4.0, 6.0, -0.0, -0.5, -1.0, -1.5, -2.0, -3.0, -4.0, -6.0])


def pack_weight(w, fmt):
    k, n = w.shape
    w = f64(bf(w)).reshape(k // 32, 32, n)
    amax = np.abs(w).max(1)
    if fmt == "e4m3":
        byte = np.frexp(amax)[1] - 1 + 127 - 7
    else:
        mant, ex = np.frexp(amax / 6.0)
        byte = np.where(mant > 0.5, ex, ex - 1) + 127
    byte = np.clip(np.where(amax > 0, byte, 1), 1, 254)
    scaled = (w * np.exp2(127.0 - byte)[:, None, :]).reshape(k, n).astype(np.float32)
    by_word = np.ascontiguousarray(scaled.reshape(k // 512, 128, 4, n).transpose(0, 1, 3, 2))
    if fmt == "e4m3":
        words = by_word.astype(ml_dtypes.float8_e4m3fn).view(np.uint8)
    else:
        c = by_word.astype(ml_dtypes.float4_e2m1fn).view(np.uint8) & 0xF
        words = c[..., 0::2] | (c[..., 1::2] << 4)
    return np.ascontiguousarray(words), np.ascontiguousarray(byte.astype(np.uint8).reshape(k // 512, 16, n))


def unpack_weight(words, scales, fmt):
    g, p, n, _ = words.shape
    if fmt == "e4m3":
        vals = np.ascontiguousarray(words).view(ml_dtypes.float8_e4m3fn).astype(np.float64)
    else:
        nib = np.empty((g, p, n, 4), np.uint8)
        nib[..., 0::2] = words & 0xF
        nib[..., 1::2] = words >> 4
        vals = E2M1[nib]
    vals = vals * np.repeat(np.exp2(scales.astype(np.float64) - 127.0), 8, axis=1)[..., None]
    return vals.transpose(0, 1, 3, 2).reshape(g * 512, n)
def pack4(w):
    words, scales = pack_weight(w, "e2m1")
    return words.reshape(words.shape[0], 128, -1), scales


def unpack4(words, scales):
    return unpack_weight(words.reshape(words.shape[0], 128, -1, 2), scales, "e2m1")


B, LC, LL, LLAMA_DIM, DIM, HEADS, FF = 16, 77, 256, 512, 512, 16, 6144
EPS = 1e-5


def layernorm(x, g, b):
    m = x.mean(-1, keepdims=True)
    v = ((x - m) ** 2).mean(-1, keepdims=True)
    return (x - m) / np.sqrt(v + EPS) * g + b


def draw0():
    s, t = mx_kscale(LLAMA_DIM), mx_kscale(DIM)
    llm_embed = bf(np.random.standard_normal((B, LL, LLAMA_DIM)) * s)
    llm_proj_w = np.random.standard_normal((DIM, LLAMA_DIM)) / np.sqrt(LLAMA_DIM) / s
    llm_proj_w_words, llm_proj_w_scales = pack4(llm_proj_w.T)
    llm_proj_b = bf(0.1 * np.random.standard_normal(DIM))
    kvn_g = bf((1.0 + 0.1 * np.random.standard_normal(DIM)) * t)
    kvn_b = bf(0.1 * np.random.standard_normal(DIM) * t)
    q_w = np.random.standard_normal((DIM, DIM)) / np.sqrt(DIM) / t
    q_w_words, q_w_scales = pack4(q_w.T)
    q_b = bf(0.1 * np.random.standard_normal(DIM))
    return {
        "llm_embed": llm_embed,
        "llm_proj_w_words": llm_proj_w_words,
        "llm_proj_w_scales": llm_proj_w_scales,
        "llm_proj_b": llm_proj_b,
        "kvn_g": kvn_g,
        "kvn_b": kvn_b,
        "q_w_words": q_w_words,
        "q_w_scales": q_w_scales,
        "q_b": q_b,
    }


def core(llm_embed, llm_proj_w_words, llm_proj_w_scales, llm_proj_b, kvn_g, kvn_b, q_w_words, q_w_scales, q_b):
    llm = (mxq(f64(llm_embed), 2, "e4m3") @ unpack4(llm_proj_w_words, llm_proj_w_scales)) + f64(llm_proj_b)
    llm_n = layernorm(llm, f64(kvn_g), f64(kvn_b))
    q = (mxq(llm_n, 2, "e4m3") @ unpack4(q_w_words, q_w_scales)) + f64(q_b)
    return llm, q


def e4m3fn_bytes(y):
    return np.clip(np.asarray(y, np.float64), -448.0, 448.0).astype(np.float32).astype(ml_dtypes.float8_e4m3fn).view(np.uint8)


def e4m3fn_values(b):
    return np.asarray(b, np.uint8).view(ml_dtypes.float8_e4m3fn).astype(np.float64)


def setup_inputs():
    d = draw0()
    x0 = np.asarray(d['llm_embed']).astype(np.float64)
    s = (np.max(np.abs(x0), axis=(0, 1), keepdims=True) / 448.0).astype(np.float32)
    out = {}
    for k, v in d.items():
        if k == 'llm_embed':
            out['llm_embed_bytes'] = e4m3fn_bytes(x0 / s.astype(np.float64))
            out['llm_embed_scale'] = s
        else:
            out[k] = v
    return out


def reference(llm_embed_bytes, llm_embed_scale, llm_proj_w_words, llm_proj_w_scales, llm_proj_b, kvn_g, kvn_b, q_w_words, q_w_scales, q_b):
    return core(e4m3fn_values(llm_embed_bytes) * llm_embed_scale.astype(np.float64), llm_proj_w_words, llm_proj_w_scales, llm_proj_b, kvn_g, kvn_b, q_w_words, q_w_scales, q_b)

@@ -1,0 +1,239 @@
+from contextlib import ExitStack
+
+import concourse.mybir as mybir
+from concourse.masks import make_identity
+
+F32 = mybir.dt.float32
+BF16 = mybir.dt.bfloat16
+U8 = mybir.dt.uint8
+U32 = mybir.dt.uint32
+I32 = mybir.dt.int32
+FP8 = mybir.dt.float8_e4m3fn
+FP8X4 = mybir.dt.float8_e4m3fn_x4
+FP4X4 = mybir.dt.float4_e2m1fn_x4
+ALU = mybir.AluOpType
+ACT = mybir.ActivationFunctionType
+
+P = 128
+TOKENS = 4096
+K = 512
+N = 512
+PACK = 4
+NT = TOKENS // P
+NPAIR = NT // 2
+EPS = 1e-5
+FLOPS = 2 * 2 * TOKENS * K * N
+
+CHUNKS = ((0, 1), (1, 1), (2, 2), (4, 4), (8, 4), (12, 4))
+
+
+def tile_crossfusion_pa_t_w4_kernel(
+    tc, x_bytes, x_scale, w1_words, w1_scales, b1, kvn_g, kvn_b, wq_words, wq_scales, bq, out_0, out_1
+):
+    nc = tc.nc
+    x_rows = x_bytes.rearrange("b l k -> (b l) k").rearrange("(p n) k -> p n k", p=P)
+    llm_rows = out_0.rearrange("b l n -> (b l) n").rearrange("(p j) n -> p j n", p=P)
+    q_rows = out_1.rearrange("b l n -> (b l) n").rearrange("(p j) n -> p j n", p=P)
+
+    with ExitStack() as ctx:
+        keep = ctx.enter_context(tc.tile_pool(name="keep", bufs=1))
+        work = ctx.enter_context(tc.tile_pool(name="work", bufs=3))
+        outs = ctx.enter_context(tc.tile_pool(name="outs", bufs=4))
+        psum = ctx.enter_context(tc.psum_pool(name="psum", bufs=2))
+
+        x_codes = {}
+        chunk_tiles = []
+        for c, (first, count) in enumerate(CHUNKS):
+            chunk = keep.tile([P, 2 * count, K], U8, align_bytes=64, name="x_codes_%d" % c)
+            chunk_tiles.append(chunk)
+            for i in range(count):
+                x_codes[first + i] = chunk[:, 2 * i : 2 * i + 2, :]
+
+        scale_bc = keep.tile([P, K], F32, align_bytes=64)
+        b1_bc = keep.tile([P, N], BF16, align_bytes=64)
+        bq_bc = keep.tile([P, N], BF16, align_bytes=64)
+        g_raw = keep.tile([P, PACK], BF16, align_bytes=64)
+        b_raw = keep.tile([P, PACK], BF16, align_bytes=64)
+        w1 = keep.tile([P, 2 * N], U8, align_bytes=256)
+        wq = keep.tile([P, 2 * N], U8, align_bytes=256)
+        w1_sc = keep.tile([P, N], U8, align_bytes=256)
+        wq_sc = keep.tile([P, N], U8, align_bytes=256)
+        g_col = keep.tile([P, PACK], F32, align_bytes=64)
+        b_col = keep.tile([P, PACK], F32, align_bytes=64)
+        eps = keep.tile([P, 1], F32, align_bytes=64)
+        warm = keep.tile([P, 1], F32, align_bytes=64)
+        ident = keep.tile([P, P], F32, align_bytes=256)
+
+        def load_x(c):
+            first, count = CHUNKS[c]
+            nc.sync.dma_start(out=chunk_tiles[c][:], in_=x_rows[:, 2 * first : 2 * (first + count), :])
+
+        def load_weight(words_tile, scales_tile, words, scales):
+            nc.sync.dma_start(out=words_tile[:], in_=words[0])
+            for r in range(4):
+                nc.sync.dma_start(
+                    out=scales_tile[r:P:32, :].bitcast(I32), in_=scales[0, r:16:4, :].bitcast(I32)
+                )
+
+        nc.vector.memset(eps[:], EPS)
+        nc.vector.memset(w1_sc[:].bitcast(I32), 0)
+        nc.vector.memset(wq_sc[:].bitcast(I32), 0)
+        nc.scalar.dma_start(out=scale_bc[:], in_=x_scale.rearrange("a b k -> (a b k)").partition_broadcast(P))
+        load_x(0)
+        load_weight(w1, w1_sc, w1_words, w1_scales)
+        nc.scalar.dma_start(out=b1_bc[:], in_=b1.partition_broadcast(P))
+        nc.scalar.dma_start(out=g_raw[:], in_=kvn_g.rearrange("(p t) -> p t", t=PACK))
+        nc.scalar.dma_start(out=b_raw[:], in_=kvn_b.rearrange("(p t) -> p t", t=PACK))
+        nc.scalar.dma_start(out=bq_bc[:], in_=bq.partition_broadcast(P))
+        nc.scalar.activation(warm[:], eps[:], ACT.Abs_reciprocal_sqrt)
+        load_x(1)
+        load_x(2)
+        load_weight(wq, wq_sc, wq_words, wq_scales)
+        for c in range(3, len(CHUNKS)):
+            load_x(c)
+        make_identity(nc, ident[:])
+
+        xt, xg, xq, xs = {}, {}, {}, {}
+        xb, acc, llm, sums, ssq, rstd, negmean = {}, {}, {}, {}, {}, {}, {}
+        z, zt, planes, ng, nq, ns, acc2 = {}, {}, {}, {}, {}, {}, {}
+
+        def widen(i):
+            xb[i] = work.tile([P, 2, K], BF16, align_bytes=64, name="xb")
+            for j in range(2):
+                nc.vector.tensor_tensor(
+                    out=xb[i][:, j, :], in0=x_codes[i][:, j, :].bitcast(FP8), in1=scale_bc[:], op=ALU.mult
+                )
+
+        def turn_x(i):
+            xt[i] = psum.tile([P, 2, 2, P], F32, name="xt")
+            words = xb[i][:].rearrange("p j k -> p (j k)").bitcast(F32)
+            for j in range(2):
+                for u in range(2):
+                    nc.tensor.transpose(xt[i][:, j, u, :], words[:, 256 * j + u : 256 * (j + 1) : 2], ident[:])
+
+        def empty_x(i):
+            xg[i] = work.tile([P, 2 * P * PACK], BF16, align_bytes=64, name="xg")
+            nc.scalar.copy(
+                xg[i][:].bitcast(F32).rearrange("p (j r u) -> p j r u", j=2, u=2),
+                xt[i][:].rearrange("p j u r -> p j r u"),
+            )
+
+        def quantise(codes, scales, src):
+            nc.vector.quantize_mx(out=codes[:].bitcast(FP8X4), scales=scales[:], in_=src[:])
+
+        def quantise_x(i):
+            xq[i] = work.tile([P, 2 * P], U32, align_bytes=256, name="xq")
+            xs[i] = work.tile([P, 2 * P], U8, align_bytes=256, name="xs")
+            quantise(xq[i], xs[i], xg[i])
+
+        def multiply(out, codes, scales, j, words, word_scales):
+            cols = slice(P * j, P * (j + 1))
+            nc.tensor.matmul_mx(
+                out=out,
+                lhsT=codes[:, cols].bitcast(FP8X4),
+                lhsT_scale=scales[:, cols],
+                rhs=words[:].bitcast(FP4X4),
+                rhs_scale=word_scales[:],
+                start=True,
+                stop=True,
+            )
+
+        def project(i):
+            for j in range(2):
+                acc[i, j] = psum.tile([P, N], F32, name="acc")
+                multiply(acc[i, j][:], xq[i], xs[i], j, w1, w1_sc)
+
+        def add_b1(i):
+            llm[i] = outs.tile([P, 2, N], F32, align_bytes=64, name="llm")
+            sums[i] = work.tile([P, 2], F32, align_bytes=64, name="sums")
+            for j in range(2):
+                nc.vector.scalar_tensor_tensor(
+                    out=llm[i][:, j, :], in0=acc[i, j][:], scalar=1.0, in1=b1_bc[:],
+                    op0=ALU.mult, op1=ALU.add, accum_out=sums[i][:, j : j + 1],
+                )
+
+        def store_llm(i):
+            nc.sync.dma_start(out=llm_rows[:, 2 * i : 2 * i + 2, :], in_=llm[i][:])
+
+        def mean(i):
+            negmean[i] = work.tile([P, 2], F32, align_bytes=64, name="negmean")
+            nc.gpsimd.tensor_scalar(
+                out=negmean[i][:], in0=sums[i][:], scalar1=-1.0 / N, scalar2=0.0, op0=ALU.mult, op1=ALU.add
+            )
+
+        def deviations(i):
+            ssq[i] = work.tile([P, 2], F32, align_bytes=64, name="ssq")
+            for j in range(2):
+                waste = work.tile([P, N], BF16, align_bytes=64, name="waste")
+                nc.scalar.activation(
+                    waste[:], llm[i][:, j, :], ACT.Square, bias=sums[i][:, j : j + 1], scale=-float(N),
+                    accum_out=ssq[i][:, j : j + 1],
+                )
+
+        def inverse_std(i):
+            rstd[i] = work.tile([P, 2], F32, align_bytes=64, name="rstd")
+            nc.scalar.activation(
+                rstd[i][:], ssq[i][:], ACT.Abs_reciprocal_sqrt, bias=eps[:], scale=1.0 / float(N * N * N)
+            )
+
+        def normalise(i):
+            z[i] = work.tile([P, 2, PACK, P], F32, align_bytes=64, name="z")
+            for j in range(2):
+                nc.gpsimd.tensor_scalar(
+                    out=z[i][:, j], in0=llm[i][:, j, :].rearrange("p (m t) -> p t m", t=PACK),
+                    scalar1=negmean[i][:, j : j + 1], scalar2=rstd[i][:, j : j + 1], op0=ALU.add, op1=ALU.mult,
+                )
+
+        def turn_z(i):
+            zt[i] = [psum.tile([P, 2, 2, P], F32, bufs=1, name="zt%d" % h) for h in range(2)]
+            for t in range(PACK):
+                for j in range(2):
+                    nc.tensor.transpose(zt[i][t // 2][:, t % 2, j, :], z[i][:, j, t, :], ident[:])
+
+        def gain(i):
+            planes[i] = work.tile([P, PACK, 2 * P], BF16, align_bytes=64, name="planes")
+            for t in range(PACK):
+                nc.scalar.activation(
+                    planes[i][:, t, :], zt[i][t // 2][:, t % 2].rearrange("p j r -> p (j r)"), ACT.Identity,
+                    bias=b_col[:, t : t + 1], scale=g_col[:, t : t + 1],
+                )
+
+        def interleave(i):
+            ng[i] = work.tile([P, 2 * P * PACK], BF16, align_bytes=64, name="ng")
+            dst = ng[i][:].rearrange("p (c t) -> p c t", t=PACK)
+            src = planes[i][:].rearrange("p t c -> p c t")
+            nc.scalar.copy(dst, src)
+
+        def quantise_n(i):
+            nq[i] = work.tile([P, 2 * P], U32, align_bytes=256, name="nq")
+            ns[i] = work.tile([P, 2 * P], U8, align_bytes=256, name="ns")
+            quantise(nq[i], ns[i], ng[i])
+
+        def query(i):
+            for j in range(2):
+                acc2[i, j] = psum.tile([P, N], F32, name="acc2")
+                multiply(acc2[i, j][:], nq[i], ns[i], j, wq, wq_sc)
+
+        def add_bq(i):
+            q = outs.tile([P, 2, N], F32, align_bytes=64, name="q")
+            for j in range(2):
+                nc.vector.tensor_tensor(out=q[:, j, :], in0=acc2[i, j][:], in1=bq_bc[:], op=ALU.add)
+            nc.sync.dma_start(out=q_rows[:, 2 * i : 2 * i + 2, :], in_=q[:])
+
+        steps = (
+            (gain, -2), (interleave, -2),
+            (widen, 2), (turn_x, 2), (empty_x, 2),
+            (quantise_x, 1),
+            (quantise_n, -3), (query, -3),
+            (add_b1, 0), (store_llm, 0), (mean, 0), (project, 1),
+            (deviations, 0), (inverse_std, 0),
+            (normalise, -1), (turn_z, -1),
+            (add_bq, -3),
+        )
+        for k in range(-2, NPAIR + 3):
+            if k == 0:
+                nc.vector.tensor_copy(out=g_col[:], in_=g_raw[:])
+                nc.vector.tensor_copy(out=b_col[:], in_=b_raw[:])
+            for stage, ahead in steps:
+                if 0 <= k + ahead < NPAIR:
+                    stage(k + ahead)

@@ -40,6 +40,7 @@ def tile_crossfusion_pa_t_w4_kernel(
         work = ctx.enter_context(tc.tile_pool(name="work", bufs=3))
         outs = ctx.enter_context(tc.tile_pool(name="outs", bufs=4))
         psum = ctx.enter_context(tc.psum_pool(name="psum", bufs=2))
+        ctx.enter_context(tc.manual_schedule())
 
         x_codes = {}
         chunk_tiles = []
@@ -94,7 +95,7 @@ def tile_crossfusion_pa_t_w4_kernel(
         make_identity(nc, ident[:])
 
         xt, xg, xq, xs = {}, {}, {}, {}
-        xb, acc, llm, sums, ssq, rstd, negmean = {}, {}, {}, {}, {}, {}, {}
+        xb, acc, llm, sums, ssq, rstd, means = {}, {}, {}, {}, {}, {}, {}
         z, zt, planes, ng, nq, ns, acc2 = {}, {}, {}, {}, {}, {}, {}
 
         def widen(i):
@@ -156,10 +157,8 @@ def tile_crossfusion_pa_t_w4_kernel(
             nc.sync.dma_start(out=llm_rows[:, 2 * i : 2 * i + 2, :], in_=llm[i][:])
 
         def mean(i):
-            negmean[i] = work.tile([P, 2], F32, align_bytes=64, name="negmean")
-            nc.gpsimd.tensor_scalar(
-                out=negmean[i][:], in0=sums[i][:], scalar1=-1.0 / N, scalar2=0.0, op0=ALU.mult, op1=ALU.add
-            )
+            means[i] = work.tile([P, 2], F32, align_bytes=64, name="means")
+            nc.scalar.activation(means[i][:], sums[i][:], ACT.Copy, scale=1.0 / N)
 
         def deviations(i):
             ssq[i] = work.tile([P, 2], F32, align_bytes=64, name="ssq")
@@ -179,9 +178,9 @@ def tile_crossfusion_pa_t_w4_kernel(
         def normalise(i):
             z[i] = work.tile([P, 2, PACK, P], F32, align_bytes=64, name="z")
             for j in range(2):
-                nc.gpsimd.tensor_scalar(
-                    out=z[i][:, j], in0=llm[i][:, j, :].rearrange("p (m t) -> p t m", t=PACK),
-                    scalar1=negmean[i][:, j : j + 1], scalar2=rstd[i][:, j : j + 1], op0=ALU.add, op1=ALU.mult,
+                nc.vector.tensor_scalar(
+                    out=z[i][:, j].rearrange("p t m -> p m t"), in0=llm[i][:, j, :].rearrange("p (m t) -> p m t", t=PACK),
+                    scalar1=means[i][:, j : j + 1], scalar2=rstd[i][:, j : j + 1], op0=ALU.subtract, op1=ALU.mult,
                 )
 
         def turn_z(i):
@@ -200,8 +199,8 @@ def tile_crossfusion_pa_t_w4_kernel(
 
         def interleave(i):
             ng[i] = work.tile([P, 2 * P * PACK], BF16, align_bytes=64, name="ng")
-            dst = ng[i][:].rearrange("p (c t) -> p c t", t=PACK)
-            src = planes[i][:].rearrange("p t c -> p c t")
+            dst = ng[i][:].rearrange("p (c i t) -> p c t i", i=4, t=PACK)
+            src = planes[i][:].rearrange("p t (c i) -> p c t i", i=4)
             nc.scalar.copy(dst, src)
 
         def quantise_n(i):
@@ -221,16 +220,11 @@ def tile_crossfusion_pa_t_w4_kernel(
             nc.sync.dma_start(out=q_rows[:, 2 * i : 2 * i + 2, :], in_=q[:])
 
         steps = (
-            (gain, -2), (interleave, -2),
-            (widen, 2), (turn_x, 2), (empty_x, 2),
-            (quantise_x, 1),
-            (quantise_n, -3), (query, -3),
-            (add_b1, 0), (store_llm, 0), (mean, 0), (project, 1),
-            (deviations, 0), (inverse_std, 0),
-            (normalise, -1), (turn_z, -1),
-            (add_bq, -3),
+            (widen, 3), (interleave, -3), (add_b1, 0), (store_llm, 0), (empty_x, 2), (inverse_std, -1),
+            (quantise_x, 1), (gain, -2), (add_bq, -4), (mean, 0), (deviations, 0), (normalise, -1),
+            (turn_x, 3), (project, 1), (turn_z, -1), (quantise_n, -3), (query, -3),
         )
-        for k in range(-2, NPAIR + 3):
+        for k in range(-3, NPAIR + 4):
             if k == 0:
                 nc.vector.tensor_copy(out=g_col[:], in_=g_raw[:])
                 nc.vector.tensor_copy(out=b_col[:], in_=b_raw[:])

@@ -38,6 +38,7 @@ def tile_crossfusion_pa_t_w4_kernel(
     with ExitStack() as ctx:
         keep = ctx.enter_context(tc.tile_pool(name="keep", bufs=1))
         work = ctx.enter_context(tc.tile_pool(name="work", bufs=3))
+        small = ctx.enter_context(tc.tile_pool(name="small", bufs=5))
         outs = ctx.enter_context(tc.tile_pool(name="outs", bufs=4))
         psum = ctx.enter_context(tc.psum_pool(name="psum", bufs=2))
         ctx.enter_context(tc.manual_schedule())
@@ -95,7 +96,7 @@ def tile_crossfusion_pa_t_w4_kernel(
         make_identity(nc, ident[:])
 
         xt, xg, xq, xs = {}, {}, {}, {}
-        xb, acc, llm, sums, ssq, rstd, means = {}, {}, {}, {}, {}, {}, {}
+        xb, acc, llm, sums, ssq, rstd, negmean, shift = {}, {}, {}, {}, {}, {}, {}, {}
         z, zt, planes, ng, nq, ns, acc2 = {}, {}, {}, {}, {}, {}, {}
 
         def widen(i):
@@ -146,7 +147,7 @@ def tile_crossfusion_pa_t_w4_kernel(
 
         def add_b1(i):
             llm[i] = outs.tile([P, 2, N], F32, align_bytes=64, name="llm")
-            sums[i] = work.tile([P, 2], F32, align_bytes=64, name="sums")
+            sums[i] = small.tile([P, 2], F32, align_bytes=64, name="sums")
             for j in range(2):
                 nc.vector.scalar_tensor_tensor(
                     out=llm[i][:, j, :], in0=acc[i, j][:], scalar=1.0, in1=b1_bc[:],
@@ -156,12 +157,18 @@ def tile_crossfusion_pa_t_w4_kernel(
         def store_llm(i):
             nc.sync.dma_start(out=llm_rows[:, 2 * i : 2 * i + 2, :], in_=llm[i][:])
 
-        def mean(i):
-            means[i] = work.tile([P, 2], F32, align_bytes=64, name="means")
-            nc.scalar.activation(means[i][:], sums[i][:], ACT.Copy, scale=1.0 / N)
+        def negative_mean(i):
+            negmean[i] = small.tile([P, 2], F32, align_bytes=64, name="negmean")
+            nc.gpsimd.tensor_scalar(
+                out=negmean[i][:], in0=sums[i][:], scalar1=-1.0 / N, scalar2=0.0, op0=ALU.mult, op1=ALU.add
+            )
+
+        def shift_of(i):
+            shift[i] = small.tile([P, 2], F32, align_bytes=64, name="shift")
+            nc.gpsimd.tensor_tensor(out=shift[i][:], in0=negmean[i][:], in1=rstd[i][:], op=ALU.mult)
 
         def deviations(i):
-            ssq[i] = work.tile([P, 2], F32, align_bytes=64, name="ssq")
+            ssq[i] = small.tile([P, 2], F32, align_bytes=64, name="ssq")
             for j in range(2):
                 waste = work.tile([P, N], BF16, align_bytes=64, name="waste")
                 nc.scalar.activation(
@@ -170,7 +177,7 @@ def tile_crossfusion_pa_t_w4_kernel(
                 )
 
         def inverse_std(i):
-            rstd[i] = work.tile([P, 2], F32, align_bytes=64, name="rstd")
+            rstd[i] = small.tile([P, 2], F32, align_bytes=64, name="rstd")
             nc.scalar.activation(
                 rstd[i][:], ssq[i][:], ACT.Abs_reciprocal_sqrt, bias=eps[:], scale=1.0 / float(N * N * N)
             )
@@ -178,10 +185,15 @@ def tile_crossfusion_pa_t_w4_kernel(
         def normalise(i):
             z[i] = work.tile([P, 2, PACK, P], F32, align_bytes=64, name="z")
             for j in range(2):
-                nc.vector.tensor_scalar(
-                    out=z[i][:, j].rearrange("p t m -> p m t"), in0=llm[i][:, j, :].rearrange("p (m t) -> p m t", t=PACK),
-                    scalar1=means[i][:, j : j + 1], scalar2=rstd[i][:, j : j + 1], op0=ALU.subtract, op1=ALU.mult,
-                )
+                dst = z[i][:, j].rearrange("p t m -> p m t")
+                src = llm[i][:, j, :].rearrange("p (m t) -> p m t", t=PACK)
+                scale, bias = rstd[i][:, j : j + 1], shift[i][:, j : j + 1]
+                if i % 4 == 2:
+                    nc.vector.tensor_scalar(
+                        out=dst, in0=src, scalar1=scale, scalar2=bias, op0=ALU.mult, op1=ALU.add
+                    )
+                else:
+                    nc.scalar.activation(dst, src, ACT.Identity, bias=bias, scale=scale)
 
         def turn_z(i):
             zt[i] = [psum.tile([P, 2, 2, P], F32, bufs=1, name="zt%d" % h) for h in range(2)]
@@ -199,9 +211,19 @@ def tile_crossfusion_pa_t_w4_kernel(
 
         def interleave(i):
             ng[i] = work.tile([P, 2 * P * PACK], BF16, align_bytes=64, name="ng")
-            dst = ng[i][:].rearrange("p (c i t) -> p c t i", i=4, t=PACK)
-            src = planes[i][:].rearrange("p t (c i) -> p c t i", i=4)
-            nc.scalar.copy(dst, src)
+            for j in range(2):
+                half = ng[i][:, j * P * PACK : (j + 1) * P * PACK]
+                cols = planes[i][:, :, j * P : (j + 1) * P]
+                if i >= NPAIR - 3:
+                    nc.vector.tensor_copy(
+                        out=half.rearrange("p (c i t) -> p c t i", i=4, t=PACK),
+                        in_=cols.rearrange("p t (c i) -> p c t i", i=4),
+                    )
+                else:
+                    nc.gpsimd.tensor_scalar(
+                        out=half.rearrange("p (c t) -> p c t", t=PACK), in0=cols.rearrange("p t c -> p c t"),
+                        scalar1=1.0, scalar2=0.0, op0=ALU.mult, op1=ALU.add,
+                    )
 
         def quantise_n(i):
             nq[i] = work.tile([P, 2 * P], U32, align_bytes=256, name="nq")
@@ -220,11 +242,11 @@ def tile_crossfusion_pa_t_w4_kernel(
             nc.sync.dma_start(out=q_rows[:, 2 * i : 2 * i + 2, :], in_=q[:])
 
         steps = (
-            (widen, 3), (interleave, -3), (add_b1, 0), (store_llm, 0), (empty_x, 2), (inverse_std, -1),
-            (quantise_x, 1), (gain, -2), (add_bq, -4), (mean, 0), (deviations, 0), (normalise, -1),
-            (turn_x, 3), (project, 1), (turn_z, -1), (quantise_n, -3), (query, -3),
+            (shift_of, -2), (negative_mean, -1), (add_b1, 0), (store_llm, 0), (deviations, -1), (quantise_n, -4),
+            (gain, -3), (turn_x, 2), (query, -5), (quantise_x, 1), (project, 1), (normalise, -2), (widen, 3),
+            (inverse_std, -1), (empty_x, 2), (add_bq, -5), (interleave, -3), (turn_z, -2),
         )
-        for k in range(-3, NPAIR + 4):
+        for k in range(-3, NPAIR + 5):
             if k == 0:
                 nc.vector.tensor_copy(out=g_col[:], in_=g_raw[:])
                 nc.vector.tensor_copy(out=b_col[:], in_=b_raw[:])

@@ -51,7 +51,10 @@ def tile_crossfusion_pa_t_w4_kernel(
             for i in range(count):
                 x_codes[first + i] = chunk[:, 2 * i : 2 * i + 2, :]
 
-        scale_bc = keep.tile([P, K], F32, align_bytes=64)
+        scale_col = keep.tile([P, PACK], F32, align_bytes=64)
+        scale_bc = keep.tile([P, 2, K], F32, align_bytes=64)
+        rows = keep.tile([P, 2, N], BF16, align_bytes=256)
+        ones = keep.tile([P, P], BF16, align_bytes=256)
         b1_bc = keep.tile([P, N], BF16, align_bytes=64)
         bq_bc = keep.tile([P, N], BF16, align_bytes=64)
         g_raw = keep.tile([P, PACK], BF16, align_bytes=64)
@@ -71,39 +74,56 @@ def tile_crossfusion_pa_t_w4_kernel(
             nc.sync.dma_start(out=chunk_tiles[c][:], in_=x_rows[:, 2 * first : 2 * (first + count), :])
 
         def load_weight(words_tile, scales_tile, words, scales):
-            nc.sync.dma_start(out=words_tile[:], in_=words[0])
             for r in range(4):
                 nc.sync.dma_start(
                     out=scales_tile[r:P:32, :].bitcast(I32), in_=scales[0, r:16:4, :].bitcast(I32)
                 )
+            nc.sync.dma_start(out=words_tile[:], in_=words[0])
 
+        nc.sync.dma_start(out=scale_col[:], in_=x_scale.rearrange("a b (p c) -> p (a b c)", c=PACK))
+        load_x(0)
+        make_identity(nc, ident[:])
         nc.vector.memset(eps[:], EPS)
         nc.vector.memset(w1_sc[:].bitcast(I32), 0)
+        nc.vector.memset(rows[:].rearrange("p h n -> p (h n)").bitcast(I32), 0)
+        nc.vector.memset(ones[:], 1.0)
         nc.vector.memset(wq_sc[:].bitcast(I32), 0)
-        nc.scalar.dma_start(out=scale_bc[:], in_=x_scale.rearrange("a b k -> (a b k)").partition_broadcast(P))
-        load_x(0)
         load_weight(w1, w1_sc, w1_words, w1_scales)
-        nc.scalar.dma_start(out=b1_bc[:], in_=b1.partition_broadcast(P))
+        nc.scalar.dma_start(out=rows[0:1, 0, :], in_=b1.rearrange("(o n) -> o n", o=1))
+        nc.scalar.activation(warm[:], eps[:], ACT.Abs_reciprocal_sqrt)
+        nc.scalar.dma_start(out=rows[0:1, 1, :], in_=bq.rearrange("(o n) -> o n", o=1))
         nc.scalar.dma_start(out=g_raw[:], in_=kvn_g.rearrange("(p t) -> p t", t=PACK))
         nc.scalar.dma_start(out=b_raw[:], in_=kvn_b.rearrange("(p t) -> p t", t=PACK))
-        nc.scalar.dma_start(out=bq_bc[:], in_=bq.partition_broadcast(P))
-        nc.scalar.activation(warm[:], eps[:], ACT.Abs_reciprocal_sqrt)
         load_x(1)
         load_x(2)
         load_weight(wq, wq_sc, wq_words, wq_scales)
         for c in range(3, len(CHUNKS)):
             load_x(c)
-        make_identity(nc, ident[:])
+
+        spread = psum.tile([P, PACK, P], F32, name="xt")
+        for c in range(PACK):
+            nc.tensor.transpose(spread[:, c, :], scale_col[:, c : c + 1].to_broadcast([P, P]), ident[:])
+        for j in range(2):
+            nc.scalar.copy(
+                scale_bc[:, j, :].rearrange("p (r c) -> p r c", c=PACK), spread[:].rearrange("p c r -> p r c")
+            )
+
+        def spread_bias(dst, row, tag):
+            bias = psum.tile([P, N], F32, name=tag)
+            nc.tensor.matmul(bias[:], lhsT=ones[:], rhs=rows[:, row, :], start=True, stop=True)
+            nc.scalar.copy(dst[:], bias[:])
 
         xt, xg, xq, xs = {}, {}, {}, {}
-        xb, acc, llm, sums, ssq, rstd, negmean, shift = {}, {}, {}, {}, {}, {}, {}, {}
-        z, zt, planes, ng, nq, ns, acc2 = {}, {}, {}, {}, {}, {}, {}
+        xb, acc, llm, sums, ssq, rstd, shift = {}, {}, {}, {}, {}, {}, {}
+        z, zt, planes, ng, nq, ns, acc2, q = {}, {}, {}, {}, {}, {}, {}, {}
 
         def widen(i):
             xb[i] = work.tile([P, 2, K], BF16, align_bytes=64, name="xb")
-            for j in range(2):
+            for cols in ([slice(0, 1), slice(1, 2)] if i == 0 else [slice(0, 2)]):
                 nc.vector.tensor_tensor(
-                    out=xb[i][:, j, :], in0=x_codes[i][:, j, :].bitcast(FP8), in1=scale_bc[:], op=ALU.mult
+                    out=xb[i][:, cols, :].rearrange("p j k -> p (j k)"),
+                    in0=x_codes[i][:, cols, :].rearrange("p j k -> p (j k)").bitcast(FP8),
+                    in1=scale_bc[:, cols, :].rearrange("p j k -> p (j k)"), op=ALU.mult,
                 )
 
         def turn_x(i):
@@ -130,42 +150,38 @@ def tile_crossfusion_pa_t_w4_kernel(
 
         def multiply(out, codes, scales, j, words, word_scales):
             cols = slice(P * j, P * (j + 1))
-            nc.tensor.matmul_mx(
-                out=out,
-                lhsT=codes[:, cols].bitcast(FP8X4),
-                lhsT_scale=scales[:, cols],
-                rhs=words[:].bitcast(FP4X4),
-                rhs_scale=word_scales[:],
-                start=True,
-                stop=True,
-            )
+            for repeat in range(2):
+                nc.tensor.matmul_mx(
+                    out=out,
+                    lhsT=codes[:, cols].bitcast(FP8X4),
+                    lhsT_scale=scales[:, cols],
+                    rhs=words[:].bitcast(FP4X4),
+                    rhs_scale=word_scales[:],
+                    start=True,
+                    stop=True,
+                )
 
         def project(i):
             for j in range(2):
                 acc[i, j] = psum.tile([P, N], F32, name="acc")
                 multiply(acc[i, j][:], xq[i], xs[i], j, w1, w1_sc)
 
-        def add_b1(i):
-            llm[i] = outs.tile([P, 2, N], F32, align_bytes=64, name="llm")
-            sums[i] = small.tile([P, 2], F32, align_bytes=64, name="sums")
-            for j in range(2):
-                nc.vector.scalar_tensor_tensor(
-                    out=llm[i][:, j, :], in0=acc[i, j][:], scalar=1.0, in1=b1_bc[:],
-                    op0=ALU.mult, op1=ALU.add, accum_out=sums[i][:, j : j + 1],
-                )
-
-        def store_llm(i):
-            nc.sync.dma_start(out=llm_rows[:, 2 * i : 2 * i + 2, :], in_=llm[i][:])
-
-        def negative_mean(i):
-            negmean[i] = small.tile([P, 2], F32, align_bytes=64, name="negmean")
-            nc.gpsimd.tensor_scalar(
-                out=negmean[i][:], in0=sums[i][:], scalar1=-1.0 / N, scalar2=0.0, op0=ALU.mult, op1=ALU.add
+        def add_b1(i, j):
+            if j == 0:
+                llm[i] = outs.tile([P, 2, N], F32, align_bytes=64, name="llm")
+                sums[i] = small.tile([P, 2], F32, align_bytes=64, name="sums")
+            nc.vector.scalar_tensor_tensor(
+                out=llm[i][:, j, :], in0=acc[i, j][:], scalar=1.0, in1=b1_bc[:],
+                op0=ALU.mult, op1=ALU.add, accum_out=sums[i][:, j : j + 1],
             )
+            if j == 1:
+                nc.sync.dma_start(out=llm_rows[:, 2 * i : 2 * i + 2, :], in_=llm[i][:])
 
         def shift_of(i):
             shift[i] = small.tile([P, 2], F32, align_bytes=64, name="shift")
-            nc.gpsimd.tensor_tensor(out=shift[i][:], in0=negmean[i][:], in1=rstd[i][:], op=ALU.mult)
+            nc.vector.scalar_tensor_tensor(
+                out=shift[i][:], in0=sums[i][:], scalar=-1.0 / N, in1=rstd[i][:], op0=ALU.mult, op1=ALU.mult
+            )
 
         def deviations(i):
             ssq[i] = small.tile([P, 2], F32, align_bytes=64, name="ssq")
@@ -204,13 +220,17 @@ def tile_crossfusion_pa_t_w4_kernel(
         def gain(i):
             planes[i] = work.tile([P, PACK, 2 * P], BF16, align_bytes=64, name="planes")
             for t in range(PACK):
-                nc.scalar.activation(
-                    planes[i][:, t, :], zt[i][t // 2][:, t % 2].rearrange("p j r -> p (j r)"), ACT.Identity,
-                    bias=b_col[:, t : t + 1], scale=g_col[:, t : t + 1],
-                )
+                src = zt[i][t // 2][:, t % 2].rearrange("p j r -> p (j r)")
+                scale, bias = g_col[:, t : t + 1], b_col[:, t : t + 1]
+                if i >= 99:
+                    nc.vector.tensor_scalar(
+                        out=planes[i][:, t, :], in0=src, scalar1=scale, scalar2=bias, op0=ALU.mult, op1=ALU.add
+                    )
+                else:
+                    nc.scalar.activation(planes[i][:, t, :], src, ACT.Identity, bias=bias, scale=scale)
 
         def interleave(i):
-            ng[i] = work.tile([P, 2 * P * PACK], BF16, align_bytes=64, name="ng")
+            ng[i] = work.tile([P, 2 * P * PACK], BF16, bufs=1, align_bytes=64, name="ng")
             for j in range(2):
                 half = ng[i][:, j * P * PACK : (j + 1) * P * PACK]
                 cols = planes[i][:, :, j * P : (j + 1) * P]
@@ -230,26 +250,32 @@ def tile_crossfusion_pa_t_w4_kernel(
             ns[i] = work.tile([P, 2 * P], U8, align_bytes=256, name="ns")
             quantise(nq[i], ns[i], ng[i])
 
-        def query(i):
-            for j in range(2):
-                acc2[i, j] = psum.tile([P, N], F32, name="acc2")
-                multiply(acc2[i, j][:], nq[i], ns[i], j, wq, wq_sc)
+        def query(i, j):
+            acc2[i, j] = psum.tile([P, N], F32, name="acc2")
+            multiply(acc2[i, j][:], nq[i], ns[i], j, wq, wq_sc)
 
-        def add_bq(i):
-            q = outs.tile([P, 2, N], F32, align_bytes=64, name="q")
-            for j in range(2):
-                nc.vector.tensor_tensor(out=q[:, j, :], in0=acc2[i, j][:], in1=bq_bc[:], op=ALU.add)
-            nc.sync.dma_start(out=q_rows[:, 2 * i : 2 * i + 2, :], in_=q[:])
+        def add_bq(i, j):
+            if j == 0:
+                q[i] = outs.tile([P, 2, N], F32, align_bytes=64, name="q")
+            nc.vector.tensor_tensor(out=q[i][:, j, :], in0=acc2[i, j][:], in1=bq_bc[:], op=ALU.add)
+            if i == NPAIR - 1:
+                nc.sync.dma_start(out=q_rows[:, 2 * i + j, :], in_=q[i][:, j, :])
+            elif j == 1:
+                nc.sync.dma_start(out=q_rows[:, 2 * i : 2 * i + 2, :], in_=q[i][:])
 
         steps = (
-            (shift_of, -2), (negative_mean, -1), (add_b1, 0), (store_llm, 0), (deviations, -1), (quantise_n, -4),
-            (gain, -3), (turn_x, 2), (query, -5), (quantise_x, 1), (project, 1), (normalise, -2), (widen, 3),
-            (inverse_std, -1), (empty_x, 2), (add_bq, -5), (interleave, -3), (turn_z, -2),
+            (shift_of, -2, ()), (deviations, -1, ()), (quantise_x, 1, ()), (turn_x, 3, ()), (query, -5, (0,)),
+            (empty_x, 2, ()), (add_bq, -6, (1,)), (interleave, -4, ()), (add_b1, 0, (0,)), (add_b1, 0, (1,)),
+            (turn_z, -3, ()), (normalise, -2, ()), (inverse_std, -1, ()), (widen, 4, ()), (gain, -3, ()),
+            (add_bq, -5, (0,)), (quantise_n, -4, ()), (project, 1, ()), (query, -5, (1,)),
         )
-        for k in range(-3, NPAIR + 5):
+        for k in range(-4, NPAIR + 6):
+            if k == -2:
+                spread_bias(b1_bc, 0, "acc")
             if k == 0:
+                spread_bias(bq_bc, 1, "acc2")
                 nc.vector.tensor_copy(out=g_col[:], in_=g_raw[:])
                 nc.vector.tensor_copy(out=b_col[:], in_=b_raw[:])
-            for stage, ahead in steps:
+            for stage, ahead, tiles in steps:
                 if 0 <= k + ahead < NPAIR:
-                    stage(k + ahead)
+                    stage(k + ahead, *tiles)

from contextlib import ExitStack

import concourse.mybir as mybir
from concourse.masks import make_identity

F32 = mybir.dt.float32
BF16 = mybir.dt.bfloat16
U8 = mybir.dt.uint8
U32 = mybir.dt.uint32
I32 = mybir.dt.int32
FP8 = mybir.dt.float8_e4m3fn
FP8X4 = mybir.dt.float8_e4m3fn_x4
FP4X4 = mybir.dt.float4_e2m1fn_x4
ALU = mybir.AluOpType
ACT = mybir.ActivationFunctionType

P = 128
TOKENS = 4096
K = 512
N = 512
PACK = 4
NT = TOKENS // P
NPAIR = NT // 2
EPS = 1e-5
FLOPS = 2 * 2 * TOKENS * K * N

CHUNKS = ((0, 1), (1, 1), (2, 2), (4, 4), (8, 4), (12, 4))


def tile_crossfusion_pa_t_w4_kernel(
    tc, x_bytes, x_scale, w1_words, w1_scales, b1, kvn_g, kvn_b, wq_words, wq_scales, bq, out_0, out_1
):
    nc = tc.nc
    x_rows = x_bytes.rearrange("b l k -> (b l) k").rearrange("(p n) k -> p n k", p=P)
    llm_rows = out_0.rearrange("b l n -> (b l) n").rearrange("(p j) n -> p j n", p=P)
    q_rows = out_1.rearrange("b l n -> (b l) n").rearrange("(p j) n -> p j n", p=P)

    with ExitStack() as ctx:
        keep = ctx.enter_context(tc.tile_pool(name="keep", bufs=1))
        work = ctx.enter_context(tc.tile_pool(name="work", bufs=3))
        small = ctx.enter_context(tc.tile_pool(name="small", bufs=5))
        outs = ctx.enter_context(tc.tile_pool(name="outs", bufs=4))
        psum = ctx.enter_context(tc.psum_pool(name="psum", bufs=2))
        ctx.enter_context(tc.manual_schedule())

        x_codes = {}
        chunk_tiles = []
        for c, (first, count) in enumerate(CHUNKS):
            chunk = keep.tile([P, 2 * count, K], U8, align_bytes=64, name="x_codes_%d" % c)
            chunk_tiles.append(chunk)
            for i in range(count):
                x_codes[first + i] = chunk[:, 2 * i : 2 * i + 2, :]

        scale_col = keep.tile([P, PACK], F32, align_bytes=64)
        scale_bc = keep.tile([P, 2, K], F32, align_bytes=64)
        rows = keep.tile([P, 2, N], BF16, align_bytes=256)
        ones = keep.tile([P, P], BF16, align_bytes=256)
        b1_bc = keep.tile([P, N], BF16, align_bytes=64)
        bq_bc = keep.tile([P, N], BF16, align_bytes=64)
        g_raw = keep.tile([P, PACK], BF16, align_bytes=64)
        b_raw = keep.tile([P, PACK], BF16, align_bytes=64)
        w1 = keep.tile([P, 2 * N], U8, align_bytes=256)
        wq = keep.tile([P, 2 * N], U8, align_bytes=256)
        w1_sc = keep.tile([P, N], U8, align_bytes=256)
        wq_sc = keep.tile([P, N], U8, align_bytes=256)
        g_col = keep.tile([P, PACK], F32, align_bytes=64)
        b_col = keep.tile([P, PACK], F32, align_bytes=64)
        eps = keep.tile([P, 1], F32, align_bytes=64)
        warm = keep.tile([P, 1], F32, align_bytes=64)
        ident = keep.tile([P, P], F32, align_bytes=256)

        def load_x(c):
            first, count = CHUNKS[c]
            nc.sync.dma_start(out=chunk_tiles[c][:], in_=x_rows[:, 2 * first : 2 * (first + count), :])

        def load_weight(words_tile, scales_tile, words, scales):
            for r in range(4):
                nc.sync.dma_start(
                    out=scales_tile[r:P:32, :].bitcast(I32), in_=scales[0, r:16:4, :].bitcast(I32)
                )
            nc.sync.dma_start(out=words_tile[:], in_=words[0])

        nc.sync.dma_start(out=scale_col[:], in_=x_scale.rearrange("a b (p c) -> p (a b c)", c=PACK))
        load_x(0)
        make_identity(nc, ident[:])
        nc.vector.memset(eps[:], EPS)
        nc.vector.memset(w1_sc[:].bitcast(I32), 0)
        nc.vector.memset(rows[:].rearrange("p h n -> p (h n)").bitcast(I32), 0)
        nc.vector.memset(ones[:], 1.0)
        nc.vector.memset(wq_sc[:].bitcast(I32), 0)
        load_weight(w1, w1_sc, w1_words, w1_scales)
        nc.scalar.dma_start(out=rows[0:1, 0, :], in_=b1.rearrange("(o n) -> o n", o=1))
        nc.scalar.activation(warm[:], eps[:], ACT.Abs_reciprocal_sqrt)
        nc.scalar.dma_start(out=rows[0:1, 1, :], in_=bq.rearrange("(o n) -> o n", o=1))
        nc.scalar.dma_start(out=g_raw[:], in_=kvn_g.rearrange("(p t) -> p t", t=PACK))
        nc.scalar.dma_start(out=b_raw[:], in_=kvn_b.rearrange("(p t) -> p t", t=PACK))
        load_x(1)
        load_x(2)
        load_weight(wq, wq_sc, wq_words, wq_scales)
        for c in range(3, len(CHUNKS)):
            load_x(c)

        spread = psum.tile([P, PACK, P], F32, name="xt")
        for c in range(PACK):
            nc.tensor.transpose(spread[:, c, :], scale_col[:, c : c + 1].to_broadcast([P, P]), ident[:])
        for j in range(2):
            nc.scalar.copy(
                scale_bc[:, j, :].rearrange("p (r c) -> p r c", c=PACK), spread[:].rearrange("p c r -> p r c")
            )

        def spread_bias(dst, row, tag):
            bias = psum.tile([P, N], F32, name=tag)
            nc.tensor.matmul(bias[:], lhsT=ones[:], rhs=rows[:, row, :], start=True, stop=True)
            nc.scalar.copy(dst[:], bias[:])

        xt, xg, xq, xs = {}, {}, {}, {}
        xb, acc, llm, sums, ssq, rstd, shift = {}, {}, {}, {}, {}, {}, {}
        z, zt, planes, ng, nq, ns, acc2, q = {}, {}, {}, {}, {}, {}, {}, {}

        def widen(i):
            xb[i] = work.tile([P, 2, K], BF16, align_bytes=64, name="xb")
            for cols in ([slice(0, 1), slice(1, 2)] if i == 0 else [slice(0, 2)]):
                nc.vector.tensor_tensor(
                    out=xb[i][:, cols, :].rearrange("p j k -> p (j k)"),
                    in0=x_codes[i][:, cols, :].rearrange("p j k -> p (j k)").bitcast(FP8),
                    in1=scale_bc[:, cols, :].rearrange("p j k -> p (j k)"), op=ALU.mult,
                )

        def turn_x(i):
            xt[i] = psum.tile([P, 2, 2, P], F32, name="xt")
            words = xb[i][:].rearrange("p j k -> p (j k)").bitcast(F32)
            for j in range(2):
                for u in range(2):
                    nc.tensor.transpose(xt[i][:, j, u, :], words[:, 256 * j + u : 256 * (j + 1) : 2], ident[:])

        def empty_x(i):
            xg[i] = work.tile([P, 2 * P * PACK], BF16, align_bytes=64, name="xg")
            nc.scalar.copy(
                xg[i][:].bitcast(F32).rearrange("p (j r u) -> p j r u", j=2, u=2),
                xt[i][:].rearrange("p j u r -> p j r u"),
            )

        def quantise(codes, scales, src):
            nc.vector.quantize_mx(out=codes[:].bitcast(FP8X4), scales=scales[:], in_=src[:])

        def quantise_x(i):
            xq[i] = work.tile([P, 2 * P], U32, align_bytes=256, name="xq")
            xs[i] = work.tile([P, 2 * P], U8, align_bytes=256, name="xs")
            quantise(xq[i], xs[i], xg[i])

        def multiply(out, codes, scales, j, words, word_scales):
            cols = slice(P * j, P * (j + 1))
            for repeat in range(2):
                nc.tensor.matmul_mx(
                    out=out,
                    lhsT=codes[:, cols].bitcast(FP8X4),
                    lhsT_scale=scales[:, cols],
                    rhs=words[:].bitcast(FP4X4),
                    rhs_scale=word_scales[:],
                    start=True,
                    stop=True,
                )

        def project(i):
            for j in range(2):
                acc[i, j] = psum.tile([P, N], F32, name="acc")
                multiply(acc[i, j][:], xq[i], xs[i], j, w1, w1_sc)

        def add_b1(i, j):
            if j == 0:
                llm[i] = outs.tile([P, 2, N], F32, align_bytes=64, name="llm")
                sums[i] = small.tile([P, 2], F32, align_bytes=64, name="sums")
            nc.vector.scalar_tensor_tensor(
                out=llm[i][:, j, :], in0=acc[i, j][:], scalar=1.0, in1=b1_bc[:],
                op0=ALU.mult, op1=ALU.add, accum_out=sums[i][:, j : j + 1],
            )
            if j == 1:
                nc.sync.dma_start(out=llm_rows[:, 2 * i : 2 * i + 2, :], in_=llm[i][:])

        def shift_of(i):
            shift[i] = small.tile([P, 2], F32, align_bytes=64, name="shift")
            nc.vector.scalar_tensor_tensor(
                out=shift[i][:], in0=sums[i][:], scalar=-1.0 / N, in1=rstd[i][:], op0=ALU.mult, op1=ALU.mult
            )

        def deviations(i):
            ssq[i] = small.tile([P, 2], F32, align_bytes=64, name="ssq")
            for j in range(2):
                waste = work.tile([P, N], BF16, align_bytes=64, name="waste")
                nc.scalar.activation(
                    waste[:], llm[i][:, j, :], ACT.Square, bias=sums[i][:, j : j + 1], scale=-float(N),
                    accum_out=ssq[i][:, j : j + 1],
                )

        def inverse_std(i):
            rstd[i] = small.tile([P, 2], F32, align_bytes=64, name="rstd")
            nc.scalar.activation(
                rstd[i][:], ssq[i][:], ACT.Abs_reciprocal_sqrt, bias=eps[:], scale=1.0 / float(N * N * N)
            )

        def normalise(i):
            z[i] = work.tile([P, 2, PACK, P], F32, align_bytes=64, name="z")
            for j in range(2):
                dst = z[i][:, j].rearrange("p t m -> p m t")
                src = llm[i][:, j, :].rearrange("p (m t) -> p m t", t=PACK)
                scale, bias = rstd[i][:, j : j + 1], shift[i][:, j : j + 1]
                if i % 4 == 2:
                    nc.vector.tensor_scalar(
                        out=dst, in0=src, scalar1=scale, scalar2=bias, op0=ALU.mult, op1=ALU.add
                    )
                else:
                    nc.scalar.activation(dst, src, ACT.Identity, bias=bias, scale=scale)

        def turn_z(i):
            zt[i] = [psum.tile([P, 2, 2, P], F32, bufs=1, name="zt%d" % h) for h in range(2)]
            for t in range(PACK):
                for j in range(2):
                    nc.tensor.transpose(zt[i][t // 2][:, t % 2, j, :], z[i][:, j, t, :], ident[:])

        def gain(i):
            planes[i] = work.tile([P, PACK, 2 * P], BF16, align_bytes=64, name="planes")
            for t in range(PACK):
                src = zt[i][t // 2][:, t % 2].rearrange("p j r -> p (j r)")
                scale, bias = g_col[:, t : t + 1], b_col[:, t : t + 1]
                if i >= 99:
                    nc.vector.tensor_scalar(
                        out=planes[i][:, t, :], in0=src, scalar1=scale, scalar2=bias, op0=ALU.mult, op1=ALU.add
                    )
                else:
                    nc.scalar.activation(planes[i][:, t, :], src, ACT.Identity, bias=bias, scale=scale)

        def interleave(i):
            ng[i] = work.tile([P, 2 * P * PACK], BF16, bufs=1, align_bytes=64, name="ng")
            for j in range(2):
                half = ng[i][:, j * P * PACK : (j + 1) * P * PACK]
                cols = planes[i][:, :, j * P : (j + 1) * P]
                if i >= NPAIR - 3:
                    nc.vector.tensor_copy(
                        out=half.rearrange("p (c i t) -> p c t i", i=4, t=PACK),
                        in_=cols.rearrange("p t (c i) -> p c t i", i=4),
                    )
                else:
                    nc.gpsimd.tensor_scalar(
                        out=half.rearrange("p (c t) -> p c t", t=PACK), in0=cols.rearrange("p t c -> p c t"),
                        scalar1=1.0, scalar2=0.0, op0=ALU.mult, op1=ALU.add,
                    )

        def quantise_n(i):
            nq[i] = work.tile([P, 2 * P], U32, align_bytes=256, name="nq")
            ns[i] = work.tile([P, 2 * P], U8, align_bytes=256, name="ns")
            quantise(nq[i], ns[i], ng[i])

        def query(i, j):
            acc2[i, j] = psum.tile([P, N], F32, name="acc2")
            multiply(acc2[i, j][:], nq[i], ns[i], j, wq, wq_sc)

        def add_bq(i, j):
            if j == 0:
                q[i] = outs.tile([P, 2, N], F32, align_bytes=64, name="q")
            nc.vector.tensor_tensor(out=q[i][:, j, :], in0=acc2[i, j][:], in1=bq_bc[:], op=ALU.add)
            if i == NPAIR - 1:
                nc.sync.dma_start(out=q_rows[:, 2 * i + j, :], in_=q[i][:, j, :])
            elif j == 1:
                nc.sync.dma_start(out=q_rows[:, 2 * i : 2 * i + 2, :], in_=q[i][:])

        steps = (
            (shift_of, -2, ()), (deviations, -1, ()), (quantise_x, 1, ()), (turn_x, 3, ()), (query, -5, (0,)),
            (empty_x, 2, ()), (add_bq, -6, (1,)), (interleave, -4, ()), (add_b1, 0, (0,)), (add_b1, 0, (1,)),
            (turn_z, -3, ()), (normalise, -2, ()), (inverse_std, -1, ()), (widen, 4, ()), (gain, -3, ()),
            (add_bq, -5, (0,)), (quantise_n, -4, ()), (project, 1, ()), (query, -5, (1,)),
        )
        for k in range(-4, NPAIR + 6):
            if k == -2:
                spread_bias(b1_bc, 0, "acc")
            if k == 0:
                spread_bias(bq_bc, 1, "acc2")
                nc.vector.tensor_copy(out=g_col[:], in_=g_raw[:])
                nc.vector.tensor_copy(out=b_col[:], in_=b_raw[:])
            for stage, ahead, tiles in steps:
                if 0 <= k + ahead < NPAIR:
                    stage(k + ahead, *tiles)
